import numpy as np
import ml_dtypes


def mxq(x, axis, fmt="e4m3"):
    dtype, down = {"e4m3": (ml_dtypes.float8_e4m3fn, 7), "e5m2": (ml_dtypes.float8_e5m2, 14)}[fmt]
    v = np.moveaxis(np.asarray(x, np.float32).astype(ml_dtypes.bfloat16).astype(np.float64), axis, -1)
    blocks = v.reshape(v.shape[:-1] + (-1, 32))
    amax = np.abs(blocks).max(-1, keepdims=True)
    byte = np.maximum(np.where(amax > 0, np.frexp(amax)[1] - 1 + 127, 0) - down, 1)
    scale = np.exp2(byte - 127.0)
    codes = (blocks / scale).astype(np.float32).astype(dtype).astype(np.float64)
    return np.moveaxis((codes * scale).reshape(v.shape), -1, axis)


WIDE = False


def mx_kscale(k):
    if not WIDE:
        return np.ones(k)
    levels = np.array([10, -10, 5, -5, 0])
    a = np.random.permutation(np.resize(levels, k // 512 * 4)).reshape(k // 512, 4)
    idx = np.arange(k)
    return np.exp2(a[idx // 512, idx % 128 // 32])


BF16 = ml_dtypes.bfloat16


def bf(x):
    return np.asarray(x, np.float32).astype(BF16)


def f64(x):
    return np.asarray(x).astype(np.float64)


B, IM, HID, L = 4096, 1024, 1024, 128


def relu(v):
    return np.maximum(v, 0.0)


def setup_inputs():
    s, t = mx_kscale(IM), mx_kscale(HID)
    return {"x": bf(np.random.random((B, IM)) * s),
            "eps": bf(np.random.standard_normal((B, L))),
            "W11": bf(np.random.standard_normal((IM, HID)) * np.sqrt(3.0 / IM) / s[:, None] * t),
            "b11": bf(np.random.standard_normal(HID) * 0.2 * t),
            "W31": bf(np.random.standard_normal((HID, L)) * np.sqrt(2.0 / HID) / t[:, None]),
            "b31": bf(np.random.standard_normal(L) * 0.2),
            "W32": bf(np.random.standard_normal((HID, L)) * np.sqrt(2.0 / HID) / t[:, None]),
            "b32": bf(np.random.standard_normal(L) * 0.2)}


def reference(x, eps, W11, b11, W31, b31, W32, b32):
    enc = relu((mxq(f64(x), 1, "e4m3") @ mxq(f64(W11), 0, "e4m3")) + f64(b11))
    encq = mxq(enc, 1, "e4m3")
    mu = relu((encq @ mxq(f64(W31), 0, "e4m3")) + f64(b31))
    sigma = relu((encq @ mxq(f64(W32), 0, "e4m3")) + f64(b32))
    z = f64(eps) * sigma + mu
    return mu, sigma, z

@@ -1,0 +1,263 @@
+from contextlib import ExitStack
+
+import concourse.mybir as mybir
+from concourse.masks import make_identity
+
+F32 = mybir.dt.float32
+BF16 = mybir.dt.bfloat16
+U32 = mybir.dt.uint32
+U8 = mybir.dt.uint8
+FP8X4 = mybir.dt.float8_e4m3fn_x4
+ALU = mybir.AluOpType
+ACT = mybir.ActivationFunctionType
+
+B, IM, HID, L = 4096, 1024, 1024, 128
+FLOPS = 2 * B * IM * HID + 2 * 2 * B * HID * L
+
+P = 128
+PACK = 4
+K_PASS = P * PACK
+PASSES = IM // K_PASS
+BANK = 512
+CHUNK = 512
+N_CHUNKS = B // CHUNK
+ROW_TILES = CHUNK // P
+HID_TILES = HID // P
+HALF = HID // 2
+
+
+def tile_mae_pa_t_kernel(tc, x, eps, W11, b11, W31, b31, W32, b32, out_0, out_1, out_2):
+    nc = tc.nc
+    with ExitStack() as ctx:
+        const = ctx.enter_context(tc.tile_pool(name="const", bufs=1))
+        stage = ctx.enter_context(tc.tile_pool(name="stage", bufs=2))
+        store = ctx.enter_context(tc.tile_pool(name="store", bufs=3))
+        psum = ctx.enter_context(tc.psum_pool(name="psum", bufs=8))
+
+        def load_x(c):
+            x_rows = const.tile([P, ROW_TILES * IM], BF16, name="x_rows%d" % c)
+            nc.sync.dma_start(
+                out=x_rows[:],
+                in_=x[c * CHUNK : (c + 1) * CHUNK, :].rearrange("(p r) k -> p (r k)", r=ROW_TILES),
+            )
+            return x_rows
+
+        x_tiles = {0: load_x(0)}
+
+        w1_raw = const.tile([P, PASSES, PACK, HID], BF16)
+        for g in range(PASSES):
+            for u in range(2):
+                first = g * K_PASS + u * 2 * P
+                nc.sync.dma_start(
+                    out=w1_raw[:, g, 2 * u : 2 * u + 2, :],
+                    in_=W11[first : first + 2 * P, :].rearrange("(q e) c -> q e c", e=2),
+                )
+
+        b11_rows = const.tile([P, P], BF16)
+        nc.vector.memset(b11_rows[:], 0.0)
+        nc.sync.dma_start(out=b11_rows[0:HID_TILES, :], in_=b11.rearrange("(h m) -> h m", m=P))
+
+        x_tiles[1] = load_x(1)
+
+        w3_raw = const.tile([P, PASSES, PACK, 2 * L], BF16)
+        nc.sync.dma_start(out=w3_raw[:, :, :, 0:L], in_=W31.rearrange("(g t p) n -> p g t n", t=PACK, p=P))
+        nc.sync.dma_start(out=w3_raw[:, :, :, L : 2 * L], in_=W32.rearrange("(g t p) n -> p g t n", t=PACK, p=P))
+
+        b3_row = const.tile([P, 2 * L], BF16)
+        nc.vector.memset(b3_row[:], 0.0)
+        nc.sync.dma_start(out=b3_row[0:1, 0:L], in_=b31.rearrange("(o n) -> o n", o=1))
+        nc.sync.dma_start(out=b3_row[0:1, L : 2 * L], in_=b32.rearrange("(o n) -> o n", o=1))
+
+        eps_sb = const.tile([P, N_CHUNKS, ROW_TILES * L], BF16)
+        nc.sync.dma_start(out=eps_sb[:], in_=eps.rearrange("(c p r) l -> p c (r l)", p=P, r=ROW_TILES))
+
+        for c in range(2, N_CHUNKS):
+            x_tiles[c] = load_x(c)
+
+        ident = const.tile([P, P], F32)
+        make_identity(nc, ident[:])
+        ones = const.tile([P, P], BF16)
+        nc.vector.memset(ones[:], 1.0)
+
+        x_codes, x_scales = {}, {}
+        enc_planes, enc_grouped, enc_codes, enc_scales = {}, {}, {}, {}
+        heads_psum, heads_pre = {}, {}
+
+        def transpose_x(c):
+            words = x_tiles[c][:].bitcast(F32)
+            grouped = stage.tile([P, PASSES * CHUNK * PACK], BF16, name="x_grouped", align_bytes=64)
+            grouped_words = grouped[:].bitcast(F32)
+            for g in range(PASSES):
+                for pair in range(ROW_TILES // 2):
+                    bank = psum.tile([P, BANK], F32, name="x_t", tag="bank")
+                    for rr in range(2):
+                        for u in range(2):
+                            first = (2 * pair + rr) * (IM // 2) + (2 * g + u) * P
+                            nc.tensor.transpose(
+                                bank[:, (2 * rr + u) * P : (2 * rr + u + 1) * P],
+                                words[:, first : first + P],
+                                ident[:],
+                            )
+                    first = (g * (ROW_TILES // 2) + pair) * BANK
+                    nc.scalar.copy(
+                        out=grouped_words[:, first : first + BANK].rearrange("p (rr c u) -> p rr c u", rr=2, u=2),
+                        in_=bank[:].rearrange("p (rr u c) -> p rr c u", rr=2, u=2),
+                    )
+            return grouped
+
+        def quantise_x(c, grouped):
+            codes = stage.tile([P, PASSES * CHUNK], U32, name="x_codes", align_bytes=64)
+            scales = stage.tile([P, PASSES * CHUNK], U8, name="x_scales", align_bytes=64)
+            nc.vector.quantize_mx(out=codes[:].bitcast(FP8X4), scales=scales[:], in_=grouped[:])
+            x_codes[c], x_scales[c] = codes, scales
+
+        def stage1(c):
+            for g2 in range(PASSES):
+                planes = stage.tile([P, PACK, CHUNK], BF16, name="enc_planes%d" % g2)
+                enc_planes[c, g2] = planes
+                for t in range(PACK):
+                    h = g2 * PACK + t
+                    h_cols = slice(h * P, (h + 1) * P)
+                    acc = psum.tile([P, BANK], F32, name="enc_acc", tag="bank")
+                    for g in range(PASSES):
+                        b_cols = slice(g * CHUNK, (g + 1) * CHUNK)
+                        nc.tensor.matmul_mx(
+                            out=acc[:],
+                            lhsT=w1_codes[:, g, h_cols].bitcast(FP8X4),
+                            lhsT_scale=w1_scales[:, g, h_cols],
+                            rhs=x_codes[c][:, b_cols].bitcast(FP8X4),
+                            rhs_scale=x_scales[c][:, b_cols],
+                            start=(g == 0),
+                            stop=(g == PASSES - 1),
+                        )
+                    nc.scalar.activation(out=planes[:, t, :], in_=acc[:], func=ACT.Relu, bias=b11_col[:, h : h + 1], scale=1.0)
+
+        def regroup(dst, src):
+            nc.vector.tensor_copy(
+                out=dst.rearrange("p (c i) t -> p c t i", i=4),
+                in_=src.rearrange("p t (c i) -> p c t i", i=4),
+            )
+
+        def regroup_enc(c, g2):
+            if g2 == 0:
+                enc_grouped[c] = stage.tile([P, PASSES, CHUNK, PACK], BF16, name="enc_grouped", align_bytes=64)
+            regroup(enc_grouped[c][:, g2], enc_planes[c, g2][:])
+
+        def quantise_enc(c):
+            codes = stage.tile([P, PASSES, CHUNK], U32, name="enc_codes", align_bytes=64)
+            scales = stage.tile([P, PASSES, CHUNK], U8, name="enc_scales", align_bytes=64)
+            nc.vector.quantize_mx(
+                out=codes[:].rearrange("p g w -> p (g w)").bitcast(FP8X4),
+                scales=scales[:].rearrange("p g w -> p (g w)"),
+                in_=enc_grouped[c][:].rearrange("p g w t -> p (g w t)"),
+            )
+            enc_codes[c], enc_scales[c] = codes, scales
+
+        def stage2(c):
+            heads_psum[c] = []
+            for pair in range(ROW_TILES // 2):
+                acc = psum.tile([P, BANK], F32, name="heads_acc", tag="bank")
+                heads_psum[c].append(acc)
+                for rr in range(2):
+                    r_cols = slice((2 * pair + rr) * P, (2 * pair + rr + 1) * P)
+                    for g2 in range(PASSES):
+                        n_cols = slice(g2 * 2 * L, (g2 + 1) * 2 * L)
+                        nc.tensor.matmul_mx(
+                            out=acc[:, rr * 2 * L : (rr + 1) * 2 * L],
+                            lhsT=enc_codes[c][:, g2, r_cols].bitcast(FP8X4),
+                            lhsT_scale=enc_scales[c][:, g2, r_cols],
+                            rhs=w3_codes[:, n_cols].bitcast(FP8X4),
+                            rhs_scale=w3_scales[:, n_cols],
+                            start=(g2 == 0),
+                            stop=(g2 == PASSES - 1),
+                        )
+
+        def add_head_bias(c):
+            pre = stage.tile([P, 2, ROW_TILES, L], F32, name="heads_pre")
+            heads_pre[c] = pre
+            for pair in range(ROW_TILES // 2):
+                nc.vector.tensor_tensor(
+                    out=pre[:, :, 2 * pair : 2 * pair + 2, :].rearrange("p s rr l -> p rr s l"),
+                    in0=heads_psum[c][pair][:].rearrange("p (rr s l) -> p rr s l", rr=2, s=2),
+                    in1=b3_all[:].unsqueeze(1).to_broadcast([P, 2, 2, L]),
+                    op=ALU.add,
+                )
+
+        def finish(c):
+            pre = heads_pre[c]
+            results = store.tile([P, 3, ROW_TILES * L], F32, name="results")
+            scaled = stage.tile([P, ROW_TILES * L], F32, name="scaled_noise")
+            pre_mu = pre[:, 0].rearrange("p r l -> p (r l)")
+            pre_sigma = pre[:, 1].rearrange("p r l -> p (r l)")
+            nc.vector.scalar_tensor_tensor(out=scaled[:], in0=pre_sigma, scalar=0.0, in1=eps_sb[:, c, :], op0=ALU.max, op1=ALU.mult)
+            nc.vector.tensor_scalar_max(
+                out=results[:, 0:2, :].rearrange("p s n -> p (s n)"),
+                in0=pre[:].rearrange("p s r l -> p (s r l)"),
+                scalar1=0.0,
+            )
+            nc.vector.scalar_tensor_tensor(out=results[:, 2, :], in0=pre_mu, scalar=0.0, in1=scaled[:], op0=ALU.max, op1=ALU.add)
+            rows = slice(c * CHUNK, (c + 1) * CHUNK)
+            for s, out in enumerate((out_0, out_1, out_2)):
+                nc.sync.dma_start(out=out[rows, :].rearrange("(p r) l -> p (r l)", r=ROW_TILES), in_=results[:, s, :])
+
+        x_grouped = {0: transpose_x(0)}
+
+        w1_codes = const.tile([P, PASSES, HID], U32, align_bytes=64)
+        w1_scales = const.tile([P, PASSES, HID], U8, align_bytes=64)
+        for half in range(2):
+            cols = slice(half * HALF, (half + 1) * HALF)
+            for g in range(PASSES):
+                w1_grouped = stage.tile([P, HALF, PACK], BF16, name="w1_grouped", align_bytes=64)
+                regroup(w1_grouped[:], w1_raw[:, g, :, cols])
+                nc.vector.quantize_mx(
+                    out=w1_codes[:, g, cols].bitcast(FP8X4),
+                    scales=w1_scales[:, g, cols],
+                    in_=w1_grouped[:].rearrange("p c t -> p (c t)"),
+                )
+            if half == 0:
+                quantise_x(0, x_grouped[0])
+
+        b11_rows_f32 = const.tile([P, P], F32)
+        nc.vector.tensor_copy(out=b11_rows_f32[:], in_=b11_rows[:])
+        b11_bank = psum.tile([P, BANK], F32, name="b11_bank", tag="bank")
+        nc.tensor.transpose(b11_bank[:, 0:P], b11_rows_f32[:], ident[:])
+        b11_col = const.tile([P, HID_TILES], F32)
+        nc.vector.tensor_copy(out=b11_col[:], in_=b11_bank[:, 0:HID_TILES])
+
+        w3_grouped = const.tile([P, PASSES, 2 * L, PACK], BF16, align_bytes=64)
+        for g2 in range(PASSES):
+            regroup(w3_grouped[:, g2], w3_raw[:, g2])
+        w3_codes = const.tile([P, PASSES * 2 * L], U32, align_bytes=64)
+        w3_scales = const.tile([P, PASSES * 2 * L], U8, align_bytes=64)
+        nc.vector.quantize_mx(
+            out=w3_codes[:].bitcast(FP8X4),
+            scales=w3_scales[:],
+            in_=w3_grouped[:].rearrange("p g n t -> p (g n t)"),
+        )
+
+        b3_bank = psum.tile([P, BANK], F32, name="b3_bank", tag="bank")
+        nc.tensor.matmul(out=b3_bank[:, 0 : 2 * L], lhsT=ones[:], rhs=b3_row[:], start=True, stop=True)
+        b3_all = const.tile([P, 2, L], F32)
+        nc.vector.tensor_copy(out=b3_all[:].rearrange("p s l -> p (s l)"), in_=b3_bank[:, 0 : 2 * L])
+
+        def exists(c):
+            return 0 <= c < N_CHUNKS
+
+        for c in range(N_CHUNKS + 2):
+            if exists(c + 1):
+                x_grouped[c + 1] = transpose_x(c + 1)
+            if exists(c - 1):
+                regroup_enc(c - 1, 1)
+            if exists(c - 2):
+                add_head_bias(c - 2)
+            if exists(c - 1):
+                quantise_enc(c - 1)
+            if exists(c - 2):
+                finish(c - 2)
+            if exists(c + 1):
+                quantise_x(c + 1, x_grouped[c + 1])
+            if exists(c):
+                stage1(c)
+                regroup_enc(c, 0)
+            if exists(c - 1):
+                stage2(c - 1)

@@ -31,8 +31,12 @@ def tile_mae_pa_t_kernel(tc, x, eps, W11, b11, W31, b31, W32, b32, out_0, out_1,
     with ExitStack() as ctx:
         const = ctx.enter_context(tc.tile_pool(name="const", bufs=1))
         stage = ctx.enter_context(tc.tile_pool(name="stage", bufs=2))
-        store = ctx.enter_context(tc.tile_pool(name="store", bufs=3))
+        store = ctx.enter_context(tc.tile_pool(name="store", bufs=2))
+        deep = ctx.enter_context(tc.tile_pool(name="deep", bufs=3))
         psum = ctx.enter_context(tc.psum_pool(name="psum", bufs=8))
+        ctx.enter_context(tc.manual_schedule())
+
+        x_tiles = {}
 
         def load_x(c):
             x_rows = const.tile([P, ROW_TILES * IM], BF16, name="x_rows%d" % c)
@@ -40,24 +44,29 @@ def tile_mae_pa_t_kernel(tc, x, eps, W11, b11, W31, b31, W32, b32, out_0, out_1,
                 out=x_rows[:],
                 in_=x[c * CHUNK : (c + 1) * CHUNK, :].rearrange("(p r) k -> p (r k)", r=ROW_TILES),
             )
-            return x_rows
+            x_tiles[c] = x_rows
 
-        x_tiles = {0: load_x(0)}
+        w1_raw = {}
 
-        w1_raw = const.tile([P, PASSES, PACK, HID], BF16)
-        for g in range(PASSES):
+        def load_w1(g, half):
+            raw = const.tile([P, PACK, HALF], BF16, name="w1_raw%d%d" % (g, half))
             for u in range(2):
                 first = g * K_PASS + u * 2 * P
                 nc.sync.dma_start(
-                    out=w1_raw[:, g, 2 * u : 2 * u + 2, :],
-                    in_=W11[first : first + 2 * P, :].rearrange("(q e) c -> q e c", e=2),
+                    out=raw[:, 2 * u : 2 * u + 2, :],
+                    in_=W11[first : first + 2 * P, half * HALF : (half + 1) * HALF].rearrange("(q e) c -> q e c", e=2),
                 )
+            w1_raw[g, half] = raw
 
+        load_w1(0, 0)
+        load_x(0)
+        load_w1(1, 0)
         b11_rows = const.tile([P, P], BF16)
         nc.vector.memset(b11_rows[:], 0.0)
         nc.sync.dma_start(out=b11_rows[0:HID_TILES, :], in_=b11.rearrange("(h m) -> h m", m=P))
-
-        x_tiles[1] = load_x(1)
+        load_w1(0, 1)
+        load_w1(1, 1)
+        load_x(1)
 
         w3_raw = const.tile([P, PASSES, PACK, 2 * L], BF16)
         nc.sync.dma_start(out=w3_raw[:, :, :, 0:L], in_=W31.rearrange("(g t p) n -> p g t n", t=PACK, p=P))
@@ -68,22 +77,22 @@ def tile_mae_pa_t_kernel(tc, x, eps, W11, b11, W31, b31, W32, b32, out_0, out_1,
         nc.sync.dma_start(out=b3_row[0:1, 0:L], in_=b31.rearrange("(o n) -> o n", o=1))
         nc.sync.dma_start(out=b3_row[0:1, L : 2 * L], in_=b32.rearrange("(o n) -> o n", o=1))
 
+        load_x(2)
         eps_sb = const.tile([P, N_CHUNKS, ROW_TILES * L], BF16)
         nc.sync.dma_start(out=eps_sb[:], in_=eps.rearrange("(c p r) l -> p c (r l)", p=P, r=ROW_TILES))
-
-        for c in range(2, N_CHUNKS):
-            x_tiles[c] = load_x(c)
+        for c in range(3, N_CHUNKS):
+            load_x(c)
 
         ident = const.tile([P, P], F32)
         make_identity(nc, ident[:])
         ones = const.tile([P, P], BF16)
         nc.vector.memset(ones[:], 1.0)
 
-        x_codes, x_scales = {}, {}
+        x_grouped, x_codes, x_scales = {}, {}, {}
         enc_planes, enc_grouped, enc_codes, enc_scales = {}, {}, {}, {}
-        heads_psum, heads_pre = {}, {}
+        heads_psum, heads_pre, results, scaled = {}, {}, {}, {}
 
-        def transpose_x(c):
+        def transpose_x(c, copies):
             words = x_tiles[c][:].bitcast(F32)
             grouped = stage.tile([P, PASSES * CHUNK * PACK], BF16, name="x_grouped", align_bytes=64)
             grouped_words = grouped[:].bitcast(F32)
@@ -99,165 +108,253 @@ def tile_mae_pa_t_kernel(tc, x, eps, W11, b11, W31, b31, W32, b32, out_0, out_1,
                                 ident[:],
                             )
                     first = (g * (ROW_TILES // 2) + pair) * BANK
-                    nc.scalar.copy(
+                    copies[pair](
                         out=grouped_words[:, first : first + BANK].rearrange("p (rr c u) -> p rr c u", rr=2, u=2),
                         in_=bank[:].rearrange("p (rr u c) -> p rr c u", rr=2, u=2),
                     )
-            return grouped
+            x_grouped[c] = grouped
 
-        def quantise_x(c, grouped):
-            codes = stage.tile([P, PASSES * CHUNK], U32, name="x_codes", align_bytes=64)
-            scales = stage.tile([P, PASSES * CHUNK], U8, name="x_scales", align_bytes=64)
-            nc.vector.quantize_mx(out=codes[:].bitcast(FP8X4), scales=scales[:], in_=grouped[:])
+        def quantise_x(c):
+            codes = deep.tile([P, PASSES * CHUNK], U32, name="x_codes", align_bytes=64)
+            scales = deep.tile([P, PASSES * CHUNK], U8, name="x_scales", align_bytes=64)
+            nc.vector.quantize_mx(out=codes[:].bitcast(FP8X4), scales=scales[:], in_=x_grouped[c][:])
             x_codes[c], x_scales[c] = codes, scales
 
-        def stage1(c):
-            for g2 in range(PASSES):
-                planes = stage.tile([P, PACK, CHUNK], BF16, name="enc_planes%d" % g2)
-                enc_planes[c, g2] = planes
-                for t in range(PACK):
-                    h = g2 * PACK + t
-                    h_cols = slice(h * P, (h + 1) * P)
-                    acc = psum.tile([P, BANK], F32, name="enc_acc", tag="bank")
-                    for g in range(PASSES):
-                        b_cols = slice(g * CHUNK, (g + 1) * CHUNK)
-                        nc.tensor.matmul_mx(
-                            out=acc[:],
-                            lhsT=w1_codes[:, g, h_cols].bitcast(FP8X4),
-                            lhsT_scale=w1_scales[:, g, h_cols],
-                            rhs=x_codes[c][:, b_cols].bitcast(FP8X4),
-                            rhs_scale=x_scales[c][:, b_cols],
-                            start=(g == 0),
-                            stop=(g == PASSES - 1),
-                        )
-                    nc.scalar.activation(out=planes[:, t, :], in_=acc[:], func=ACT.Relu, bias=b11_col[:, h : h + 1], scale=1.0)
+        def stage1(c, h):
+            g2, t = divmod(h, PACK)
+            if t == 0:
+                enc_planes[c, g2] = stage.tile([P, PACK, CHUNK], BF16, name="enc_planes%d" % g2)
+            h_cols = slice(h * P, (h + 1) * P)
+            acc = psum.tile([P, BANK], F32, name="enc_acc", tag="bank")
+            for g in range(PASSES):
+                b_cols = slice(g * CHUNK, (g + 1) * CHUNK)
+                nc.tensor.matmul_mx(
+                    out=acc[:],
+                    lhsT=w1_codes[:, g, h_cols].bitcast(FP8X4),
+                    lhsT_scale=w1_scales[:, g, h_cols],
+                    rhs=x_codes[c][:, b_cols].bitcast(FP8X4),
+                    rhs_scale=x_scales[c][:, b_cols],
+                    start=(g == 0),
+                    stop=(g == PASSES - 1),
+                )
+            nc.scalar.activation(
+                out=enc_planes[c, g2][:, t, :], in_=acc[:], func=ACT.Relu, bias=b11_col[:, h : h + 1], scale=1.0
+            )
 
-        def regroup(dst, src):
-            nc.vector.tensor_copy(
+        def regroup(dst, src, copy=nc.vector.tensor_copy):
+            copy(
                 out=dst.rearrange("p (c i) t -> p c t i", i=4),
                 in_=src.rearrange("p t (c i) -> p c t i", i=4),
             )
 
-        def regroup_enc(c, g2):
-            if g2 == 0:
+        def regroup_enc(c, g2, rows=slice(0, CHUNK)):
+            if c not in enc_grouped:
                 enc_grouped[c] = stage.tile([P, PASSES, CHUNK, PACK], BF16, name="enc_grouped", align_bytes=64)
-            regroup(enc_grouped[c][:, g2], enc_planes[c, g2][:])
+            regroup(enc_grouped[c][:, g2, rows], enc_planes[c, g2][:, :, rows])
 
-        def quantise_enc(c):
-            codes = stage.tile([P, PASSES, CHUNK], U32, name="enc_codes", align_bytes=64)
-            scales = stage.tile([P, PASSES, CHUNK], U8, name="enc_scales", align_bytes=64)
-            nc.vector.quantize_mx(
-                out=codes[:].rearrange("p g w -> p (g w)").bitcast(FP8X4),
-                scales=scales[:].rearrange("p g w -> p (g w)"),
-                in_=enc_grouped[c][:].rearrange("p g w t -> p (g w t)"),
-            )
-            enc_codes[c], enc_scales[c] = codes, scales
-
-        def stage2(c):
-            heads_psum[c] = []
-            for pair in range(ROW_TILES // 2):
-                acc = psum.tile([P, BANK], F32, name="heads_acc", tag="bank")
-                heads_psum[c].append(acc)
-                for rr in range(2):
-                    r_cols = slice((2 * pair + rr) * P, (2 * pair + rr + 1) * P)
-                    for g2 in range(PASSES):
-                        n_cols = slice(g2 * 2 * L, (g2 + 1) * 2 * L)
-                        nc.tensor.matmul_mx(
-                            out=acc[:, rr * 2 * L : (rr + 1) * 2 * L],
-                            lhsT=enc_codes[c][:, g2, r_cols].bitcast(FP8X4),
-                            lhsT_scale=enc_scales[c][:, g2, r_cols],
-                            rhs=w3_codes[:, n_cols].bitcast(FP8X4),
-                            rhs_scale=w3_scales[:, n_cols],
-                            start=(g2 == 0),
-                            stop=(g2 == PASSES - 1),
-                        )
-
-        def add_head_bias(c):
-            pre = stage.tile([P, 2, ROW_TILES, L], F32, name="heads_pre")
-            heads_pre[c] = pre
-            for pair in range(ROW_TILES // 2):
-                nc.vector.tensor_tensor(
-                    out=pre[:, :, 2 * pair : 2 * pair + 2, :].rearrange("p s rr l -> p rr s l"),
-                    in0=heads_psum[c][pair][:].rearrange("p (rr s l) -> p rr s l", rr=2, s=2),
-                    in1=b3_all[:].unsqueeze(1).to_broadcast([P, 2, 2, L]),
-                    op=ALU.add,
+        def quantise_enc(c, g2=None, rows=slice(0, CHUNK)):
+            if c not in enc_codes:
+                enc_codes[c] = deep.tile([P, PASSES, CHUNK], U32, name="enc_codes", align_bytes=64)
+                enc_scales[c] = deep.tile([P, PASSES, CHUNK], U8, name="enc_scales", align_bytes=64)
+            if g2 is None:
+                out, scales, in_ = enc_codes[c][:], enc_scales[c][:], enc_grouped[c][:]
+                nc.vector.quantize_mx(
+                    out=out.rearrange("p g w -> p (g w)").bitcast(FP8X4),
+                    scales=scales.rearrange("p g w -> p (g w)"),
+                    in_=in_.rearrange("p g w t -> p (g w t)"),
+                )
+            else:
+                nc.vector.quantize_mx(
+                    out=enc_codes[c][:, g2, rows].bitcast(FP8X4),
+                    scales=enc_scales[c][:, g2, rows],
+                    in_=enc_grouped[c][:, g2, rows].rearrange("p w t -> p (w t)"),
                 )
 
-        def finish(c):
-            pre = heads_pre[c]
-            results = store.tile([P, 3, ROW_TILES * L], F32, name="results")
-            scaled = stage.tile([P, ROW_TILES * L], F32, name="scaled_noise")
-            pre_mu = pre[:, 0].rearrange("p r l -> p (r l)")
-            pre_sigma = pre[:, 1].rearrange("p r l -> p (r l)")
-            nc.vector.scalar_tensor_tensor(out=scaled[:], in0=pre_sigma, scalar=0.0, in1=eps_sb[:, c, :], op0=ALU.max, op1=ALU.mult)
-            nc.vector.tensor_scalar_max(
-                out=results[:, 0:2, :].rearrange("p s n -> p (s n)"),
-                in0=pre[:].rearrange("p s r l -> p (s r l)"),
-                scalar1=0.0,
-            )
-            nc.vector.scalar_tensor_tensor(out=results[:, 2, :], in0=pre_mu, scalar=0.0, in1=scaled[:], op0=ALU.max, op1=ALU.add)
-            rows = slice(c * CHUNK, (c + 1) * CHUNK)
-            for s, out in enumerate((out_0, out_1, out_2)):
-                nc.sync.dma_start(out=out[rows, :].rearrange("(p r) l -> p (r l)", r=ROW_TILES), in_=results[:, s, :])
+        def stage2(c, pair):
+            acc = psum.tile([P, BANK], F32, name="heads_acc", tag="bank")
+            heads_psum[c, pair] = acc
+            for rr in range(2):
+                r_cols = slice((2 * pair + rr) * P, (2 * pair + rr + 1) * P)
+                for g2 in range(PASSES):
+                    n_cols = slice(g2 * 2 * L, (g2 + 1) * 2 * L)
+                    nc.tensor.matmul_mx(
+                        out=acc[:, rr * 2 * L : (rr + 1) * 2 * L],
+                        lhsT=enc_codes[c][:, g2, r_cols].bitcast(FP8X4),
+                        lhsT_scale=enc_scales[c][:, g2, r_cols],
+                        rhs=w3_codes[:, n_cols].bitcast(FP8X4),
+                        rhs_scale=w3_scales[:, n_cols],
+                        start=(g2 == 0),
+                        stop=(g2 == PASSES - 1),
+                    )
 
-        x_grouped = {0: transpose_x(0)}
+        def add_head_bias(c, pair):
+            if c not in heads_pre:
+                heads_pre[c] = stage.tile([P, 2, ROW_TILES, L], F32, name="heads_pre")
+                results[c] = store.tile([P, 3, ROW_TILES, L], F32, name="results")
+                scaled[c] = stage.tile([P, ROW_TILES, L], F32, name="scaled_noise")
+            nc.vector.tensor_tensor(
+                out=heads_pre[c][:, :, 2 * pair : 2 * pair + 2, :].rearrange("p s rr l -> p rr s l"),
+                in0=heads_psum[c, pair][:].rearrange("p (rr s l) -> p rr s l", rr=2, s=2),
+                in1=b3_all[:].unsqueeze(1).to_broadcast([P, 2, 2, L]),
+                op=ALU.add,
+            )
+
+        def flat(ap):
+            return ap.rearrange("p r l -> p (r l)")
+
+        def relu_mu(c, r=slice(0, ROW_TILES)):
+            nc.scalar.activation(out=flat(results[c][:, 0, r]), in_=flat(heads_pre[c][:, 0, r]), func=ACT.Relu)
+
+        def relu_sigma(c, r=slice(0, ROW_TILES)):
+            nc.vector.tensor_scalar_max(out=flat(results[c][:, 1, r]), in0=flat(heads_pre[c][:, 1, r]), scalar1=0.0)
+
+        def scale_noise(c, r=slice(0, ROW_TILES)):
+            nc.vector.scalar_tensor_tensor(
+                out=flat(scaled[c][:, r]), in0=flat(heads_pre[c][:, 1, r]), scalar=0.0,
+                in1=eps_sb[:, c, r.start * L : r.stop * L], op0=ALU.max, op1=ALU.mult,
+            )
+
+        def sample(c, r=slice(0, ROW_TILES)):
+            nc.vector.scalar_tensor_tensor(
+                out=flat(results[c][:, 2, r]), in0=flat(heads_pre[c][:, 0, r]), scalar=0.0,
+                in1=flat(scaled[c][:, r]), op0=ALU.max, op1=ALU.add,
+            )
+
+        def store_out(c, s, r=slice(0, ROW_TILES)):
+            out = (out_0, out_1, out_2)[s]
+            rows = slice(c * CHUNK, (c + 1) * CHUNK)
+            nc.sync.dma_start(
+                out=out[rows, :].rearrange("(p r) l -> p r l", r=ROW_TILES)[:, r, :], in_=results[c][:, s, r, :]
+            )
 
         w1_codes = const.tile([P, PASSES, HID], U32, align_bytes=64)
         w1_scales = const.tile([P, PASSES, HID], U8, align_bytes=64)
-        for half in range(2):
+        w1_grouped = {}
+
+        def regroup_w1(g, half, copy=nc.vector.tensor_copy):
+            w1_grouped[g, half] = stage.tile([P, HALF, PACK], BF16, name="w1_grouped%d" % half, align_bytes=64)
+            regroup(w1_grouped[g, half][:], w1_raw[g, half][:], copy)
+
+        def quantise_w1(g, half):
             cols = slice(half * HALF, (half + 1) * HALF)
-            for g in range(PASSES):
-                w1_grouped = stage.tile([P, HALF, PACK], BF16, name="w1_grouped", align_bytes=64)
-                regroup(w1_grouped[:], w1_raw[:, g, :, cols])
-                nc.vector.quantize_mx(
-                    out=w1_codes[:, g, cols].bitcast(FP8X4),
-                    scales=w1_scales[:, g, cols],
-                    in_=w1_grouped[:].rearrange("p c t -> p (c t)"),
-                )
-            if half == 0:
-                quantise_x(0, x_grouped[0])
+            nc.vector.quantize_mx(
+                out=w1_codes[:, g, cols].bitcast(FP8X4),
+                scales=w1_scales[:, g, cols],
+                in_=w1_grouped[g, half][:].rearrange("p c t -> p (c t)"),
+            )
+
+        regroup_w1(0, 0)
+        quantise_w1(0, 0)
+        transpose_x(0, (nc.scalar.copy, nc.vector.tensor_copy))
 
         b11_rows_f32 = const.tile([P, P], F32)
-        nc.vector.tensor_copy(out=b11_rows_f32[:], in_=b11_rows[:])
+        nc.scalar.copy(out=b11_rows_f32[:], in_=b11_rows[:])
         b11_bank = psum.tile([P, BANK], F32, name="b11_bank", tag="bank")
         nc.tensor.transpose(b11_bank[:, 0:P], b11_rows_f32[:], ident[:])
         b11_col = const.tile([P, HID_TILES], F32)
-        nc.vector.tensor_copy(out=b11_col[:], in_=b11_bank[:, 0:HID_TILES])
+        nc.scalar.copy(out=b11_col[:], in_=b11_bank[:, 0:HID_TILES])
+
+        regroup_w1(1, 0)
+        quantise_x(0)
+        quantise_w1(1, 0)
+        regroup_w1(0, 1, nc.scalar.copy)
+        regroup_w1(1, 1)
+        quantise_w1(0, 1)
+        quantise_w1(1, 1)
 
         w3_grouped = const.tile([P, PASSES, 2 * L, PACK], BF16, align_bytes=64)
-        for g2 in range(PASSES):
-            regroup(w3_grouped[:, g2], w3_raw[:, g2])
         w3_codes = const.tile([P, PASSES * 2 * L], U32, align_bytes=64)
         w3_scales = const.tile([P, PASSES * 2 * L], U8, align_bytes=64)
-        nc.vector.quantize_mx(
-            out=w3_codes[:].bitcast(FP8X4),
-            scales=w3_scales[:],
-            in_=w3_grouped[:].rearrange("p g n t -> p (g n t)"),
-        )
-
-        b3_bank = psum.tile([P, BANK], F32, name="b3_bank", tag="bank")
-        nc.tensor.matmul(out=b3_bank[:, 0 : 2 * L], lhsT=ones[:], rhs=b3_row[:], start=True, stop=True)
         b3_all = const.tile([P, 2, L], F32)
-        nc.vector.tensor_copy(out=b3_all[:].rearrange("p s l -> p (s l)"), in_=b3_bank[:, 0 : 2 * L])
+
+        def prepare_heads():
+            for g2 in range(PASSES):
+                regroup(w3_grouped[:, g2], w3_raw[:, g2], nc.scalar.copy)
+            nc.vector.quantize_mx(
+                out=w3_codes[:].bitcast(FP8X4),
+                scales=w3_scales[:],
+                in_=w3_grouped[:].rearrange("p g n t -> p (g n t)"),
+            )
+            b3_bank = psum.tile([P, BANK], F32, name="b3_bank", tag="bank")
+            nc.tensor.matmul(out=b3_bank[:, 0 : 2 * L], lhsT=ones[:], rhs=b3_row[:], start=True, stop=True)
+            nc.scalar.copy(out=b3_all[:].rearrange("p s l -> p (s l)"), in_=b3_bank[:, 0 : 2 * L])
 
         def exists(c):
             return 0 <= c < N_CHUNKS
 
-        for c in range(N_CHUNKS + 2):
-            if exists(c + 1):
-                x_grouped[c + 1] = transpose_x(c + 1)
-            if exists(c - 1):
+        both = (nc.scalar.copy, nc.scalar.copy)
+        for c in range(N_CHUNKS):
+            if c == 0:
+                for h in range(PACK):
+                    stage1(c, h)
+                transpose_x(1, (nc.scalar.copy, nc.vector.tensor_copy))
+                quantise_x(1)
+                for h in range(PACK, HID_TILES):
+                    stage1(c, h)
+            else:
+                if exists(c + 1):
+                    transpose_x(c + 1, both)
+                if exists(c - 3):
+                    scale_noise(c - 3)
                 regroup_enc(c - 1, 1)
-            if exists(c - 2):
-                add_head_bias(c - 2)
-            if exists(c - 1):
+                if exists(c - 3):
+                    relu_sigma(c - 3)
+                    sample(c - 3)
+                if exists(c + 1):
+                    quantise_x(c + 1)
                 quantise_enc(c - 1)
+                for h in range(PACK):
+                    stage1(c, h)
+                if exists(c - 3):
+                    relu_mu(c - 3)
+                    for s in (1, 0, 2):
+                        store_out(c - 3, s)
+                if exists(c - 2):
+                    stage2(c - 2, 0)
+                    stage2(c - 2, 1)
+                for h in range(PACK, HID_TILES):
+                    stage1(c, h)
+            if c == 1:
+                prepare_heads()
             if exists(c - 2):
-                finish(c - 2)
-            if exists(c + 1):
-                quantise_x(c + 1, x_grouped[c + 1])
-            if exists(c):
-                stage1(c)
-                regroup_enc(c, 0)
-            if exists(c - 1):
-                stage2(c - 1)
+                add_head_bias(c - 2, 0)
+                add_head_bias(c - 2, 1)
+            regroup_enc(c, 0)
+
+        a, b, last = N_CHUNKS - 3, N_CHUNKS - 2, N_CHUNKS - 1
+        pairs = [slice(0, 2), slice(2, 4)]
+        row_halves = [slice(0, CHUNK // 2), slice(CHUNK // 2, CHUNK)]
+        stage2(b, 0)
+        stage2(b, 1)
+        scale_noise(a)
+        quantise_enc(last, 0)
+        sample(a)
+        relu_sigma(a)
+        regroup_enc(last, 1, row_halves[0])
+        relu_mu(a)
+        for s in (2, 1, 0):
+            store_out(a, s)
+        add_head_bias(b, 0)
+        quantise_enc(last, 1, row_halves[0])
+        regroup_enc(last, 1, row_halves[1])
+        add_head_bias(b, 1)
+        quantise_enc(last, 1, row_halves[1])
+        stage2(last, 0)
+        stage2(last, 1)
+        relu_mu(b)
+        scale_noise(b)
+        relu_sigma(b)
+        add_head_bias(last, 0)
+        sample(b)
+        for s in (0, 1, 2):
+            store_out(b, s)
+        for p in range(2):
+            r = pairs[p]
+            scale_noise(last, r)
+            if p == 0:
+                add_head_bias(last, 1)
+            relu_mu(last, r)
+            nc.scalar.activation(out=flat(results[last][:, 1, r]), in_=flat(heads_pre[last][:, 1, r]), func=ACT.Relu)
+            sample(last, r)
+            for s in (0, 1, 2):
+                store_out(last, s, r)

@@ -38,13 +38,13 @@ def tile_mae_pa_t_kernel(tc, x, eps, W11, b11, W31, b31, W32, b32, out_0, out_1,
 
         x_tiles = {}
 
-        def load_x(c):
-            x_rows = const.tile([P, ROW_TILES * IM], BF16, name="x_rows%d" % c)
+        def load_x(c, rows=slice(0, ROW_TILES)):
+            if c not in x_tiles:
+                x_tiles[c] = const.tile([P, ROW_TILES, IM], BF16, name="x_rows%d" % c)
             nc.sync.dma_start(
-                out=x_rows[:],
-                in_=x[c * CHUNK : (c + 1) * CHUNK, :].rearrange("(p r) k -> p (r k)", r=ROW_TILES),
+                out=x_tiles[c][:, rows, :],
+                in_=x[c * CHUNK : (c + 1) * CHUNK, :].rearrange("(p r) k -> p r k", r=ROW_TILES)[:, rows, :],
             )
-            x_tiles[c] = x_rows
 
         w1_raw = {}
 
@@ -58,9 +58,11 @@ def tile_mae_pa_t_kernel(tc, x, eps, W11, b11, W31, b31, W32, b32, out_0, out_1,
                 )
             w1_raw[g, half] = raw
 
+        pairs = [slice(0, 2), slice(2, 4)]
         load_w1(0, 0)
-        load_x(0)
+        load_x(0, pairs[0])
         load_w1(1, 0)
+        load_x(0, pairs[1])
         b11_rows = const.tile([P, P], BF16)
         nc.vector.memset(b11_rows[:], 0.0)
         nc.sync.dma_start(out=b11_rows[0:HID_TILES, :], in_=b11.rearrange("(h m) -> h m", m=P))
@@ -92,12 +94,13 @@ def tile_mae_pa_t_kernel(tc, x, eps, W11, b11, W31, b31, W32, b32, out_0, out_1,
         enc_planes, enc_grouped, enc_codes, enc_scales = {}, {}, {}, {}
         heads_psum, heads_pre, results, scaled = {}, {}, {}, {}
 
-        def transpose_x(c, copies):
-            words = x_tiles[c][:].bitcast(F32)
-            grouped = stage.tile([P, PASSES * CHUNK * PACK], BF16, name="x_grouped", align_bytes=64)
-            grouped_words = grouped[:].bitcast(F32)
+        def transpose_x(c, copies, row_pairs=(0, 1)):
+            words = x_tiles[c][:].rearrange("p r k -> p (r k)").bitcast(F32)
+            if c not in x_grouped:
+                x_grouped[c] = stage.tile([P, PASSES * CHUNK * PACK], BF16, name="x_grouped", align_bytes=64)
+            grouped_words = x_grouped[c][:].bitcast(F32)
             for g in range(PASSES):
-                for pair in range(ROW_TILES // 2):
+                for pair in row_pairs:
                     bank = psum.tile([P, BANK], F32, name="x_t", tag="bank")
                     for rr in range(2):
                         for u in range(2):
@@ -108,28 +111,32 @@ def tile_mae_pa_t_kernel(tc, x, eps, W11, b11, W31, b31, W32, b32, out_0, out_1,
                                 ident[:],
                             )
                     first = (g * (ROW_TILES // 2) + pair) * BANK
-                    copies[pair](
+                    copies[(g * len(row_pairs) + pair) % 2](
                         out=grouped_words[:, first : first + BANK].rearrange("p (rr c u) -> p rr c u", rr=2, u=2),
                         in_=bank[:].rearrange("p (rr u c) -> p rr c u", rr=2, u=2),
                     )
-            x_grouped[c] = grouped
 
-        def quantise_x(c):
-            codes = deep.tile([P, PASSES * CHUNK], U32, name="x_codes", align_bytes=64)
-            scales = deep.tile([P, PASSES * CHUNK], U8, name="x_scales", align_bytes=64)
-            nc.vector.quantize_mx(out=codes[:].bitcast(FP8X4), scales=scales[:], in_=x_grouped[c][:])
-            x_codes[c], x_scales[c] = codes, scales
+        def quantise_x(c, windows=(slice(0, PASSES * CHUNK),)):
+            if c not in x_codes:
+                x_codes[c] = deep.tile([P, PASSES * CHUNK], U32, name="x_codes", align_bytes=64)
+                x_scales[c] = deep.tile([P, PASSES * CHUNK], U8, name="x_scales", align_bytes=64)
+            for w in windows:
+                nc.vector.quantize_mx(
+                    out=x_codes[c][:, w].bitcast(FP8X4),
+                    scales=x_scales[c][:, w],
+                    in_=x_grouped[c][:, PACK * w.start : PACK * w.stop],
+                )
 
-        def stage1(c, h):
-            g2, t = divmod(h, PACK)
-            if t == 0:
-                enc_planes[c, g2] = stage.tile([P, PACK, CHUNK], BF16, name="enc_planes%d" % g2)
+        enc_acc = {}
+
+        def stage1_matmul(c, h, rows=slice(0, CHUNK)):
+            if (c, h) not in enc_acc:
+                enc_acc[c, h] = psum.tile([P, BANK], F32, name="enc_acc", tag="bank")
             h_cols = slice(h * P, (h + 1) * P)
-            acc = psum.tile([P, BANK], F32, name="enc_acc", tag="bank")
             for g in range(PASSES):
-                b_cols = slice(g * CHUNK, (g + 1) * CHUNK)
+                b_cols = slice(g * CHUNK + rows.start, g * CHUNK + rows.stop)
                 nc.tensor.matmul_mx(
-                    out=acc[:],
+                    out=enc_acc[c, h][:, rows],
                     lhsT=w1_codes[:, g, h_cols].bitcast(FP8X4),
                     lhsT_scale=w1_scales[:, g, h_cols],
                     rhs=x_codes[c][:, b_cols].bitcast(FP8X4),
@@ -137,9 +144,18 @@ def tile_mae_pa_t_kernel(tc, x, eps, W11, b11, W31, b31, W32, b32, out_0, out_1,
                     start=(g == 0),
                     stop=(g == PASSES - 1),
                 )
+
+        def stage1_relu(c, h):
+            g2, t = divmod(h, PACK)
+            if t == 0:
+                enc_planes[c, g2] = stage.tile([P, PACK, CHUNK], BF16, name="enc_planes%d" % g2)
             nc.scalar.activation(
-                out=enc_planes[c, g2][:, t, :], in_=acc[:], func=ACT.Relu, bias=b11_col[:, h : h + 1], scale=1.0
+                out=enc_planes[c, g2][:, t, :], in_=enc_acc[c, h][:], func=ACT.Relu, bias=b11_col[:, h : h + 1], scale=1.0
             )
+
+        def stage1(c, h):
+            stage1_matmul(c, h)
+            stage1_relu(c, h)
 
         def regroup(dst, src, copy=nc.vector.tensor_copy):
             copy(
@@ -147,10 +163,10 @@ def tile_mae_pa_t_kernel(tc, x, eps, W11, b11, W31, b31, W32, b32, out_0, out_1,
                 in_=src.rearrange("p t (c i) -> p c t i", i=4),
             )
 
-        def regroup_enc(c, g2, rows=slice(0, CHUNK)):
+        def regroup_enc(c, g2, rows=slice(0, CHUNK), copy=nc.vector.tensor_copy):
             if c not in enc_grouped:
                 enc_grouped[c] = stage.tile([P, PASSES, CHUNK, PACK], BF16, name="enc_grouped", align_bytes=64)
-            regroup(enc_grouped[c][:, g2, rows], enc_planes[c, g2][:, :, rows])
+            regroup(enc_grouped[c][:, g2, rows], enc_planes[c, g2][:, :, rows], copy)
 
         def quantise_enc(c, g2=None, rows=slice(0, CHUNK)):
             if c not in enc_codes:
@@ -206,7 +222,10 @@ def tile_mae_pa_t_kernel(tc, x, eps, W11, b11, W31, b31, W32, b32, out_0, out_1,
             nc.scalar.activation(out=flat(results[c][:, 0, r]), in_=flat(heads_pre[c][:, 0, r]), func=ACT.Relu)
 
         def relu_sigma(c, r=slice(0, ROW_TILES)):
-            nc.vector.tensor_scalar_max(out=flat(results[c][:, 1, r]), in0=flat(heads_pre[c][:, 1, r]), scalar1=0.0)
+            if c < N_CHUNKS // 2:
+                nc.vector.tensor_scalar_max(out=flat(results[c][:, 1, r]), in0=flat(heads_pre[c][:, 1, r]), scalar1=0.0)
+            else:
+                nc.scalar.activation(out=flat(results[c][:, 1, r]), in_=flat(heads_pre[c][:, 1, r]), func=ACT.Relu)
 
         def scale_noise(c, r=slice(0, ROW_TILES)):
             nc.vector.scalar_tensor_tensor(
@@ -230,6 +249,9 @@ def tile_mae_pa_t_kernel(tc, x, eps, W11, b11, W31, b31, W32, b32, out_0, out_1,
         w1_codes = const.tile([P, PASSES, HID], U32, align_bytes=64)
         w1_scales = const.tile([P, PASSES, HID], U8, align_bytes=64)
         w1_grouped = {}
+        w3_grouped = const.tile([P, PASSES, 2 * L, PACK], BF16, align_bytes=64)
+        w3_codes = const.tile([P, PASSES * 2 * L], U32, align_bytes=64)
+        w3_scales = const.tile([P, PASSES * 2 * L], U8, align_bytes=64)
 
         def regroup_w1(g, half, copy=nc.vector.tensor_copy):
             w1_grouped[g, half] = stage.tile([P, HALF, PACK], BF16, name="w1_grouped%d" % half, align_bytes=64)
@@ -243,100 +265,113 @@ def tile_mae_pa_t_kernel(tc, x, eps, W11, b11, W31, b31, W32, b32, out_0, out_1,
                 in_=w1_grouped[g, half][:].rearrange("p c t -> p (c t)"),
             )
 
+        row_halves = [slice(0, CHUNK // 2), slice(CHUNK // 2, CHUNK)]
+
+        def windows(rows):
+            return [slice(g * CHUNK + rows.start, g * CHUNK + rows.stop) for g in range(PASSES)]
+
+        both = (nc.scalar.copy, nc.scalar.copy)
+        shared = (nc.scalar.copy, nc.vector.tensor_copy)
         regroup_w1(0, 0)
         quantise_w1(0, 0)
-        transpose_x(0, (nc.scalar.copy, nc.vector.tensor_copy))
+        transpose_x(0, both, (0,))
 
         b11_rows_f32 = const.tile([P, P], F32)
         nc.scalar.copy(out=b11_rows_f32[:], in_=b11_rows[:])
+        regroup_w1(1, 0)
+        quantise_x(0, windows(row_halves[0]))
+        quantise_w1(1, 0)
+        transpose_x(0, both, (1,))
         b11_bank = psum.tile([P, BANK], F32, name="b11_bank", tag="bank")
         nc.tensor.transpose(b11_bank[:, 0:P], b11_rows_f32[:], ident[:])
         b11_col = const.tile([P, HID_TILES], F32)
         nc.scalar.copy(out=b11_col[:], in_=b11_bank[:, 0:HID_TILES])
-
-        regroup_w1(1, 0)
-        quantise_x(0)
-        quantise_w1(1, 0)
         regroup_w1(0, 1, nc.scalar.copy)
+
+        for h in range(PACK):
+            stage1_matmul(0, h, row_halves[0])
+        quantise_x(0, windows(row_halves[1]))
+        for h in range(PACK):
+            stage1_matmul(0, h, row_halves[1])
+            stage1_relu(0, h)
         regroup_w1(1, 1)
-        quantise_w1(0, 1)
         quantise_w1(1, 1)
+        quantise_w1(0, 1)
+        transpose_x(1, shared)
+        for h in range(PACK, HID_TILES):
+            stage1(0, h)
+        quantise_x(1)
+        regroup_enc(0, 0)
 
-        w3_grouped = const.tile([P, PASSES, 2 * L, PACK], BF16, align_bytes=64)
-        w3_codes = const.tile([P, PASSES * 2 * L], U32, align_bytes=64)
-        w3_scales = const.tile([P, PASSES * 2 * L], U8, align_bytes=64)
-        b3_all = const.tile([P, 2, L], F32)
-
-        def prepare_heads():
+        def prepare_w3():
             for g2 in range(PASSES):
-                regroup(w3_grouped[:, g2], w3_raw[:, g2], nc.scalar.copy)
+                regroup(w3_grouped[:, g2], w3_raw[:, g2])
             nc.vector.quantize_mx(
                 out=w3_codes[:].bitcast(FP8X4),
                 scales=w3_scales[:],
                 in_=w3_grouped[:].rearrange("p g n t -> p (g n t)"),
             )
-            b3_bank = psum.tile([P, BANK], F32, name="b3_bank", tag="bank")
-            nc.tensor.matmul(out=b3_bank[:, 0 : 2 * L], lhsT=ones[:], rhs=b3_row[:], start=True, stop=True)
-            nc.scalar.copy(out=b3_all[:].rearrange("p s l -> p (s l)"), in_=b3_bank[:, 0 : 2 * L])
+
+        b3_all = const.tile([P, 2, L], F32)
 
         def exists(c):
             return 0 <= c < N_CHUNKS
 
-        both = (nc.scalar.copy, nc.scalar.copy)
-        for c in range(N_CHUNKS):
-            if c == 0:
-                for h in range(PACK):
-                    stage1(c, h)
-                transpose_x(1, (nc.scalar.copy, nc.vector.tensor_copy))
-                quantise_x(1)
-                for h in range(PACK, HID_TILES):
-                    stage1(c, h)
-            else:
-                if exists(c + 1):
-                    transpose_x(c + 1, both)
-                if exists(c - 3):
-                    scale_noise(c - 3)
-                regroup_enc(c - 1, 1)
-                if exists(c - 3):
-                    relu_sigma(c - 3)
-                    sample(c - 3)
-                if exists(c + 1):
-                    quantise_x(c + 1)
-                quantise_enc(c - 1)
-                for h in range(PACK):
-                    stage1(c, h)
-                if exists(c - 3):
-                    relu_mu(c - 3)
-                    for s in (1, 0, 2):
-                        store_out(c - 3, s)
-                if exists(c - 2):
-                    stage2(c - 2, 0)
-                    stage2(c - 2, 1)
-                for h in range(PACK, HID_TILES):
-                    stage1(c, h)
+        last = N_CHUNKS - 1
+        for c in range(1, N_CHUNKS):
+            if exists(c + 1) and c > 1:
+                transpose_x(c + 1, both)
+            if exists(c - 3):
+                scale_noise(c - 3)
+            regroup_enc(c - 1, 1)
+            if exists(c - 3):
+                relu_sigma(c - 3)
+                sample(c - 3)
+            quantise_enc(c - 1)
             if c == 1:
-                prepare_heads()
+                prepare_w3()
+            elif exists(c + 1):
+                quantise_x(c + 1)
+            for h in range(PACK):
+                stage1(c, h)
+            if c == 1:
+                transpose_x(2, shared)
+                quantise_x(2)
+            if exists(c - 3):
+                relu_mu(c - 3)
+                for s in (1, 0, 2):
+                    store_out(c - 3, s)
+            if exists(c - 2):
+                stage2(c - 2, 0)
+                stage2(c - 2, 1)
+            for h in range(PACK, HID_TILES):
+                stage1(c, h)
+            if c == 1:
+                b3_bank = psum.tile([P, BANK], F32, name="b3_bank", tag="bank")
+                nc.tensor.matmul(out=b3_bank[:, 0 : 2 * L], lhsT=ones[:], rhs=b3_row[:], start=True, stop=True)
+                nc.scalar.copy(out=b3_all[:].rearrange("p s l -> p (s l)"), in_=b3_bank[:, 0 : 2 * L])
             if exists(c - 2):
                 add_head_bias(c - 2, 0)
                 add_head_bias(c - 2, 1)
-            regroup_enc(c, 0)
+            if c < last:
+                regroup_enc(c, 0)
 
-        a, b, last = N_CHUNKS - 3, N_CHUNKS - 2, N_CHUNKS - 1
-        pairs = [slice(0, 2), slice(2, 4)]
-        row_halves = [slice(0, CHUNK // 2), slice(CHUNK // 2, CHUNK)]
+        a, b = N_CHUNKS - 3, N_CHUNKS - 2
+        regroup_enc(last, 0, row_halves[0])
+        regroup_enc(last, 0, row_halves[1], nc.scalar.copy)
         stage2(b, 0)
         stage2(b, 1)
         scale_noise(a)
         quantise_enc(last, 0)
         sample(a)
-        relu_sigma(a)
         regroup_enc(last, 1, row_halves[0])
+        regroup_enc(last, 1, row_halves[1], nc.scalar.copy)
         relu_mu(a)
-        for s in (2, 1, 0):
+        relu_sigma(a)
+        for s in (2, 0, 1):
             store_out(a, s)
         add_head_bias(b, 0)
         quantise_enc(last, 1, row_halves[0])
-        regroup_enc(last, 1, row_halves[1])
         add_head_bias(b, 1)
         quantise_enc(last, 1, row_halves[1])
         stage2(last, 0)
@@ -354,7 +389,7 @@ def tile_mae_pa_t_kernel(tc, x, eps, W11, b11, W31, b31, W32, b32, out_0, out_1,
             if p == 0:
                 add_head_bias(last, 1)
             relu_mu(last, r)
-            nc.scalar.activation(out=flat(results[last][:, 1, r]), in_=flat(heads_pre[last][:, 1, r]), func=ACT.Relu)
+            relu_sigma(last, r)
             sample(last, r)
             for s in (0, 1, 2):
                 store_out(last, s, r)

@@ -89,6 +89,13 @@ def tile_mae_pa_t_kernel(tc, x, eps, W11, b11, W31, b31, W32, b32, out_0, out_1,
         make_identity(nc, ident[:])
         ones = const.tile([P, P], BF16)
         nc.vector.memset(ones[:], 1.0)
+        zeros = const.tile([P, BANK], BF16)
+        nc.vector.memset(zeros[:], 0.0)
+
+        def keep_warm(n):
+            idle_bank = psum.tile([P, BANK], F32, name="idle_bank", tag="bank")
+            for i in range(n):
+                nc.tensor.matmul(out=idle_bank[:], lhsT=ones[:], rhs=zeros[:], start=True, stop=True)
 
         x_grouped, x_codes, x_scales = {}, {}, {}
         enc_planes, enc_grouped, enc_codes, enc_scales = {}, {}, {}, {}
@@ -272,9 +279,11 @@ def tile_mae_pa_t_kernel(tc, x, eps, W11, b11, W31, b31, W32, b32, out_0, out_1,
 
         both = (nc.scalar.copy, nc.scalar.copy)
         shared = (nc.scalar.copy, nc.vector.tensor_copy)
+        keep_warm(8)
         regroup_w1(0, 0)
         quantise_w1(0, 0)
         transpose_x(0, both, (0,))
+        keep_warm(2)
 
         b11_rows_f32 = const.tile([P, P], F32)
         nc.scalar.copy(out=b11_rows_f32[:], in_=b11_rows[:])
@@ -282,6 +291,7 @@ def tile_mae_pa_t_kernel(tc, x, eps, W11, b11, W31, b31, W32, b32, out_0, out_1,
         quantise_x(0, windows(row_halves[0]))
         quantise_w1(1, 0)
         transpose_x(0, both, (1,))
+        keep_warm(2)
         b11_bank = psum.tile([P, BANK], F32, name="b11_bank", tag="bank")
         nc.tensor.transpose(b11_bank[:, 0:P], b11_rows_f32[:], ident[:])
         b11_col = const.tile([P, HID_TILES], F32)

@@ -260,16 +260,22 @@ def tile_mae_pa_t_kernel(tc, x, eps, W11, b11, W31, b31, W32, b32, out_0, out_1,
         w3_codes = const.tile([P, PASSES * 2 * L], U32, align_bytes=64)
         w3_scales = const.tile([P, PASSES * 2 * L], U8, align_bytes=64)
 
-        def regroup_w1(g, half, copy=nc.vector.tensor_copy):
-            w1_grouped[g, half] = stage.tile([P, HALF, PACK], BF16, name="w1_grouped%d" % half, align_bytes=64)
-            regroup(w1_grouped[g, half][:], w1_raw[g, half][:], copy)
+        def within(quarter):
+            return slice(0, HALF) if quarter is None else slice(quarter * HALF // 2, (quarter + 1) * HALF // 2)
 
-        def quantise_w1(g, half):
-            cols = slice(half * HALF, (half + 1) * HALF)
+        def regroup_w1(g, half, copy=nc.vector.tensor_copy, quarter=None):
+            if (g, half) not in w1_grouped:
+                w1_grouped[g, half] = stage.tile([P, HALF, PACK], BF16, name="w1_grouped%d" % half, align_bytes=64)
+            cols = within(quarter)
+            regroup(w1_grouped[g, half][:, cols], w1_raw[g, half][:, :, cols], copy)
+
+        def quantise_w1(g, half, quarter=None):
+            cols = within(quarter)
+            to = slice(half * HALF + cols.start, half * HALF + cols.stop)
             nc.vector.quantize_mx(
-                out=w1_codes[:, g, cols].bitcast(FP8X4),
-                scales=w1_scales[:, g, cols],
-                in_=w1_grouped[g, half][:].rearrange("p c t -> p (c t)"),
+                out=w1_codes[:, g, to].bitcast(FP8X4),
+                scales=w1_scales[:, g, to],
+                in_=w1_grouped[g, half][:, cols].rearrange("p c t -> p (c t)"),
             )
 
         row_halves = [slice(0, CHUNK // 2), slice(CHUNK // 2, CHUNK)]
@@ -280,8 +286,10 @@ def tile_mae_pa_t_kernel(tc, x, eps, W11, b11, W31, b31, W32, b32, out_0, out_1,
         both = (nc.scalar.copy, nc.scalar.copy)
         shared = (nc.scalar.copy, nc.vector.tensor_copy)
         keep_warm(8)
-        regroup_w1(0, 0)
-        quantise_w1(0, 0)
+        for quarter in range(2):
+            regroup_w1(0, 0, nc.vector.tensor_copy, quarter)
+        for quarter in range(2):
+            quantise_w1(0, 0, quarter)
         transpose_x(0, both, (0,))
         keep_warm(2)
 
@@ -305,17 +313,15 @@ def tile_mae_pa_t_kernel(tc, x, eps, W11, b11, W31, b31, W32, b32, out_0, out_1,
             stage1_matmul(0, h, row_halves[1])
             stage1_relu(0, h)
         regroup_w1(1, 1)
-        quantise_w1(1, 1)
         quantise_w1(0, 1)
+        quantise_w1(1, 1)
         transpose_x(1, shared)
         for h in range(PACK, HID_TILES):
             stage1(0, h)
-        quantise_x(1)
         regroup_enc(0, 0)
+        quantise_x(1)
 
-        def prepare_w3():
-            for g2 in range(PASSES):
-                regroup(w3_grouped[:, g2], w3_raw[:, g2])
+        def quantise_w3():
             nc.vector.quantize_mx(
                 out=w3_codes[:].bitcast(FP8X4),
                 scales=w3_scales[:],
@@ -337,16 +343,22 @@ def tile_mae_pa_t_kernel(tc, x, eps, W11, b11, W31, b31, W32, b32, out_0, out_1,
             if exists(c - 3):
                 relu_sigma(c - 3)
                 sample(c - 3)
-            quantise_enc(c - 1)
             if c == 1:
-                prepare_w3()
+                for g2 in range(PASSES):
+                    regroup(w3_grouped[:, g2], w3_raw[:, g2])
+            if exists(c - 3):
+                quantise_enc(c - 1)
+            else:
+                for g2 in range(PASSES):
+                    quantise_enc(c - 1, g2)
+            if c == 1:
+                quantise_w3()
             elif exists(c + 1):
                 quantise_x(c + 1)
             for h in range(PACK):
                 stage1(c, h)
             if c == 1:
                 transpose_x(2, shared)
-                quantise_x(2)
             if exists(c - 3):
                 relu_mu(c - 3)
                 for s in (1, 0, 2):
@@ -365,6 +377,8 @@ def tile_mae_pa_t_kernel(tc, x, eps, W11, b11, W31, b31, W32, b32, out_0, out_1,
                 add_head_bias(c - 2, 1)
             if c < last:
                 regroup_enc(c, 0)
+            if c == 1:
+                quantise_x(2)
 
         a, b = N_CHUNKS - 3, N_CHUNKS - 2
         regroup_enc(last, 0, row_halves[0])

@@ -225,14 +225,13 @@ def tile_mae_pa_t_kernel(tc, x, eps, W11, b11, W31, b31, W32, b32, out_0, out_1,
         def flat(ap):
             return ap.rearrange("p r l -> p (r l)")
 
-        def relu_mu(c, r=slice(0, ROW_TILES)):
-            nc.scalar.activation(out=flat(results[c][:, 0, r]), in_=flat(heads_pre[c][:, 0, r]), func=ACT.Relu)
-
-        def relu_sigma(c, r=slice(0, ROW_TILES)):
+        def relu_heads(c, r=slice(0, ROW_TILES)):
+            head = heads_pre[c][:, :, r].rearrange("p s r l -> p s (r l)")
+            out = results[c][:, 0:2, r].rearrange("p s r l -> p s (r l)")
             if c < N_CHUNKS // 2:
-                nc.vector.tensor_scalar_max(out=flat(results[c][:, 1, r]), in0=flat(heads_pre[c][:, 1, r]), scalar1=0.0)
+                nc.vector.tensor_scalar_max(out=out, in0=head, scalar1=0.0)
             else:
-                nc.scalar.activation(out=flat(results[c][:, 1, r]), in_=flat(heads_pre[c][:, 1, r]), func=ACT.Relu)
+                nc.scalar.activation(out=out, in_=head, func=ACT.Relu)
 
         def scale_noise(c, r=slice(0, ROW_TILES)):
             nc.vector.scalar_tensor_tensor(
@@ -304,14 +303,13 @@ def tile_mae_pa_t_kernel(tc, x, eps, W11, b11, W31, b31, W32, b32, out_0, out_1,
         nc.tensor.transpose(b11_bank[:, 0:P], b11_rows_f32[:], ident[:])
         b11_col = const.tile([P, HID_TILES], F32)
         nc.scalar.copy(out=b11_col[:], in_=b11_bank[:, 0:HID_TILES])
-        regroup_w1(0, 1, nc.scalar.copy)
-
         for h in range(PACK):
             stage1_matmul(0, h, row_halves[0])
         quantise_x(0, windows(row_halves[1]))
         for h in range(PACK):
             stage1_matmul(0, h, row_halves[1])
             stage1_relu(0, h)
+        regroup_w1(0, 1)
         regroup_w1(1, 1)
         quantise_w1(0, 1)
         quantise_w1(1, 1)
@@ -340,8 +338,9 @@ def tile_mae_pa_t_kernel(tc, x, eps, W11, b11, W31, b31, W32, b32, out_0, out_1,
             if exists(c - 3):
                 scale_noise(c - 3)
             regroup_enc(c - 1, 1)
+            if exists(c - 3) and c - 3 < N_CHUNKS // 2:
+                relu_heads(c - 3)
             if exists(c - 3):
-                relu_sigma(c - 3)
                 sample(c - 3)
             if c == 1:
                 for g2 in range(PASSES):
@@ -360,7 +359,8 @@ def tile_mae_pa_t_kernel(tc, x, eps, W11, b11, W31, b31, W32, b32, out_0, out_1,
             if c == 1:
                 transpose_x(2, shared)
             if exists(c - 3):
-                relu_mu(c - 3)
+                if c - 3 >= N_CHUNKS // 2:
+                    relu_heads(c - 3)
                 for s in (1, 0, 2):
                     store_out(c - 3, s)
             if exists(c - 2):
@@ -390,8 +390,7 @@ def tile_mae_pa_t_kernel(tc, x, eps, W11, b11, W31, b31, W32, b32, out_0, out_1,
         sample(a)
         regroup_enc(last, 1, row_halves[0])
         regroup_enc(last, 1, row_halves[1], nc.scalar.copy)
-        relu_mu(a)
-        relu_sigma(a)
+        relu_heads(a)
         for s in (2, 0, 1):
             store_out(a, s)
         add_head_bias(b, 0)
@@ -400,9 +399,8 @@ def tile_mae_pa_t_kernel(tc, x, eps, W11, b11, W31, b31, W32, b32, out_0, out_1,
         quantise_enc(last, 1, row_halves[1])
         stage2(last, 0)
         stage2(last, 1)
-        relu_mu(b)
+        relu_heads(b)
         scale_noise(b)
-        relu_sigma(b)
         add_head_bias(last, 0)
         sample(b)
         for s in (0, 1, 2):
@@ -412,8 +410,7 @@ def tile_mae_pa_t_kernel(tc, x, eps, W11, b11, W31, b31, W32, b32, out_0, out_1,
             scale_noise(last, r)
             if p == 0:
                 add_head_bias(last, 1)
-            relu_mu(last, r)
-            relu_sigma(last, r)
+            relu_heads(last, r)
             sample(last, r)
             for s in (0, 1, 2):
                 store_out(last, s, r)

from contextlib import ExitStack

import concourse.mybir as mybir
from concourse.masks import make_identity

F32 = mybir.dt.float32
BF16 = mybir.dt.bfloat16
U32 = mybir.dt.uint32
U8 = mybir.dt.uint8
FP8X4 = mybir.dt.float8_e4m3fn_x4
ALU = mybir.AluOpType
ACT = mybir.ActivationFunctionType

B, IM, HID, L = 4096, 1024, 1024, 128
FLOPS = 2 * B * IM * HID + 2 * 2 * B * HID * L

P = 128
PACK = 4
K_PASS = P * PACK
PASSES = IM // K_PASS
BANK = 512
CHUNK = 512
N_CHUNKS = B // CHUNK
ROW_TILES = CHUNK // P
HID_TILES = HID // P
HALF = HID // 2


def tile_mae_pa_t_kernel(tc, x, eps, W11, b11, W31, b31, W32, b32, out_0, out_1, out_2):
    nc = tc.nc
    with ExitStack() as ctx:
        const = ctx.enter_context(tc.tile_pool(name="const", bufs=1))
        stage = ctx.enter_context(tc.tile_pool(name="stage", bufs=2))
        store = ctx.enter_context(tc.tile_pool(name="store", bufs=2))
        deep = ctx.enter_context(tc.tile_pool(name="deep", bufs=3))
        psum = ctx.enter_context(tc.psum_pool(name="psum", bufs=8))
        ctx.enter_context(tc.manual_schedule())

        x_tiles = {}

        def load_x(c, rows=slice(0, ROW_TILES)):
            if c not in x_tiles:
                x_tiles[c] = const.tile([P, ROW_TILES, IM], BF16, name="x_rows%d" % c)
            nc.sync.dma_start(
                out=x_tiles[c][:, rows, :],
                in_=x[c * CHUNK : (c + 1) * CHUNK, :].rearrange("(p r) k -> p r k", r=ROW_TILES)[:, rows, :],
            )

        w1_raw = {}

        def load_w1(g, half):
            raw = const.tile([P, PACK, HALF], BF16, name="w1_raw%d%d" % (g, half))
            for u in range(2):
                first = g * K_PASS + u * 2 * P
                nc.sync.dma_start(
                    out=raw[:, 2 * u : 2 * u + 2, :],
                    in_=W11[first : first + 2 * P, half * HALF : (half + 1) * HALF].rearrange("(q e) c -> q e c", e=2),
                )
            w1_raw[g, half] = raw

        pairs = [slice(0, 2), slice(2, 4)]
        load_w1(0, 0)
        load_x(0, pairs[0])
        load_w1(1, 0)
        load_x(0, pairs[1])
        b11_rows = const.tile([P, P], BF16)
        nc.vector.memset(b11_rows[:], 0.0)
        nc.sync.dma_start(out=b11_rows[0:HID_TILES, :], in_=b11.rearrange("(h m) -> h m", m=P))
        load_w1(0, 1)
        load_w1(1, 1)
        load_x(1)

        w3_raw = const.tile([P, PASSES, PACK, 2 * L], BF16)
        nc.sync.dma_start(out=w3_raw[:, :, :, 0:L], in_=W31.rearrange("(g t p) n -> p g t n", t=PACK, p=P))
        nc.sync.dma_start(out=w3_raw[:, :, :, L : 2 * L], in_=W32.rearrange("(g t p) n -> p g t n", t=PACK, p=P))

        b3_row = const.tile([P, 2 * L], BF16)
        nc.vector.memset(b3_row[:], 0.0)
        nc.sync.dma_start(out=b3_row[0:1, 0:L], in_=b31.rearrange("(o n) -> o n", o=1))
        nc.sync.dma_start(out=b3_row[0:1, L : 2 * L], in_=b32.rearrange("(o n) -> o n", o=1))

        load_x(2)
        eps_sb = const.tile([P, N_CHUNKS, ROW_TILES * L], BF16)
        nc.sync.dma_start(out=eps_sb[:], in_=eps.rearrange("(c p r) l -> p c (r l)", p=P, r=ROW_TILES))
        for c in range(3, N_CHUNKS):
            load_x(c)

        ident = const.tile([P, P], F32)
        make_identity(nc, ident[:])
        ones = const.tile([P, P], BF16)
        nc.vector.memset(ones[:], 1.0)
        zeros = const.tile([P, BANK], BF16)
        nc.vector.memset(zeros[:], 0.0)

        def keep_warm(n):
            idle_bank = psum.tile([P, BANK], F32, name="idle_bank", tag="bank")
            for i in range(n):
                nc.tensor.matmul(out=idle_bank[:], lhsT=ones[:], rhs=zeros[:], start=True, stop=True)

        x_grouped, x_codes, x_scales = {}, {}, {}
        enc_planes, enc_grouped, enc_codes, enc_scales = {}, {}, {}, {}
        heads_psum, heads_pre, results, scaled = {}, {}, {}, {}

        def transpose_x(c, copies, row_pairs=(0, 1)):
            words = x_tiles[c][:].rearrange("p r k -> p (r k)").bitcast(F32)
            if c not in x_grouped:
                x_grouped[c] = stage.tile([P, PASSES * CHUNK * PACK], BF16, name="x_grouped", align_bytes=64)
            grouped_words = x_grouped[c][:].bitcast(F32)
            for g in range(PASSES):
                for pair in row_pairs:
                    bank = psum.tile([P, BANK], F32, name="x_t", tag="bank")
                    for rr in range(2):
                        for u in range(2):
                            first = (2 * pair + rr) * (IM // 2) + (2 * g + u) * P
                            nc.tensor.transpose(
                                bank[:, (2 * rr + u) * P : (2 * rr + u + 1) * P],
                                words[:, first : first + P],
                                ident[:],
                            )
                    first = (g * (ROW_TILES // 2) + pair) * BANK
                    copies[(g * len(row_pairs) + pair) % 2](
                        out=grouped_words[:, first : first + BANK].rearrange("p (rr c u) -> p rr c u", rr=2, u=2),
                        in_=bank[:].rearrange("p (rr u c) -> p rr c u", rr=2, u=2),
                    )

        def quantise_x(c, windows=(slice(0, PASSES * CHUNK),)):
            if c not in x_codes:
                x_codes[c] = deep.tile([P, PASSES * CHUNK], U32, name="x_codes", align_bytes=64)
                x_scales[c] = deep.tile([P, PASSES * CHUNK], U8, name="x_scales", align_bytes=64)
            for w in windows:
                nc.vector.quantize_mx(
                    out=x_codes[c][:, w].bitcast(FP8X4),
                    scales=x_scales[c][:, w],
                    in_=x_grouped[c][:, PACK * w.start : PACK * w.stop],
                )

        enc_acc = {}

        def stage1_matmul(c, h, rows=slice(0, CHUNK)):
            if (c, h) not in enc_acc:
                enc_acc[c, h] = psum.tile([P, BANK], F32, name="enc_acc", tag="bank")
            h_cols = slice(h * P, (h + 1) * P)
            for g in range(PASSES):
                b_cols = slice(g * CHUNK + rows.start, g * CHUNK + rows.stop)
                nc.tensor.matmul_mx(
                    out=enc_acc[c, h][:, rows],
                    lhsT=w1_codes[:, g, h_cols].bitcast(FP8X4),
                    lhsT_scale=w1_scales[:, g, h_cols],
                    rhs=x_codes[c][:, b_cols].bitcast(FP8X4),
                    rhs_scale=x_scales[c][:, b_cols],
                    start=(g == 0),
                    stop=(g == PASSES - 1),
                )

        def stage1_relu(c, h):
            g2, t = divmod(h, PACK)
            if t == 0:
                enc_planes[c, g2] = stage.tile([P, PACK, CHUNK], BF16, name="enc_planes%d" % g2)
            nc.scalar.activation(
                out=enc_planes[c, g2][:, t, :], in_=enc_acc[c, h][:], func=ACT.Relu, bias=b11_col[:, h : h + 1], scale=1.0
            )

        def stage1(c, h):
            stage1_matmul(c, h)
            stage1_relu(c, h)

        def regroup(dst, src, copy=nc.vector.tensor_copy):
            copy(
                out=dst.rearrange("p (c i) t -> p c t i", i=4),
                in_=src.rearrange("p t (c i) -> p c t i", i=4),
            )

        def regroup_enc(c, g2, rows=slice(0, CHUNK), copy=nc.vector.tensor_copy):
            if c not in enc_grouped:
                enc_grouped[c] = stage.tile([P, PASSES, CHUNK, PACK], BF16, name="enc_grouped", align_bytes=64)
            regroup(enc_grouped[c][:, g2, rows], enc_planes[c, g2][:, :, rows], copy)

        def quantise_enc(c, g2=None, rows=slice(0, CHUNK)):
            if c not in enc_codes:
                enc_codes[c] = deep.tile([P, PASSES, CHUNK], U32, name="enc_codes", align_bytes=64)
                enc_scales[c] = deep.tile([P, PASSES, CHUNK], U8, name="enc_scales", align_bytes=64)
            if g2 is None:
                out, scales, in_ = enc_codes[c][:], enc_scales[c][:], enc_grouped[c][:]
                nc.vector.quantize_mx(
                    out=out.rearrange("p g w -> p (g w)").bitcast(FP8X4),
                    scales=scales.rearrange("p g w -> p (g w)"),
                    in_=in_.rearrange("p g w t -> p (g w t)"),
                )
            else:
                nc.vector.quantize_mx(
                    out=enc_codes[c][:, g2, rows].bitcast(FP8X4),
                    scales=enc_scales[c][:, g2, rows],
                    in_=enc_grouped[c][:, g2, rows].rearrange("p w t -> p (w t)"),
                )

        def stage2(c, pair):
            acc = psum.tile([P, BANK], F32, name="heads_acc", tag="bank")
            heads_psum[c, pair] = acc
            for rr in range(2):
                r_cols = slice((2 * pair + rr) * P, (2 * pair + rr + 1) * P)
                for g2 in range(PASSES):
                    n_cols = slice(g2 * 2 * L, (g2 + 1) * 2 * L)
                    nc.tensor.matmul_mx(
                        out=acc[:, rr * 2 * L : (rr + 1) * 2 * L],
                        lhsT=enc_codes[c][:, g2, r_cols].bitcast(FP8X4),
                        lhsT_scale=enc_scales[c][:, g2, r_cols],
                        rhs=w3_codes[:, n_cols].bitcast(FP8X4),
                        rhs_scale=w3_scales[:, n_cols],
                        start=(g2 == 0),
                        stop=(g2 == PASSES - 1),
                    )

        def add_head_bias(c, pair):
            if c not in heads_pre:
                heads_pre[c] = stage.tile([P, 2, ROW_TILES, L], F32, name="heads_pre")
                results[c] = store.tile([P, 3, ROW_TILES, L], F32, name="results")
                scaled[c] = stage.tile([P, ROW_TILES, L], F32, name="scaled_noise")
            nc.vector.tensor_tensor(
                out=heads_pre[c][:, :, 2 * pair : 2 * pair + 2, :].rearrange("p s rr l -> p rr s l"),
                in0=heads_psum[c, pair][:].rearrange("p (rr s l) -> p rr s l", rr=2, s=2),
                in1=b3_all[:].unsqueeze(1).to_broadcast([P, 2, 2, L]),
                op=ALU.add,
            )

        def flat(ap):
            return ap.rearrange("p r l -> p (r l)")

        def relu_heads(c, r=slice(0, ROW_TILES)):
            head = heads_pre[c][:, :, r].rearrange("p s r l -> p s (r l)")
            out = results[c][:, 0:2, r].rearrange("p s r l -> p s (r l)")
            if c < N_CHUNKS // 2:
                nc.vector.tensor_scalar_max(out=out, in0=head, scalar1=0.0)
            else:
                nc.scalar.activation(out=out, in_=head, func=ACT.Relu)

        def scale_noise(c, r=slice(0, ROW_TILES)):
            nc.vector.scalar_tensor_tensor(
                out=flat(scaled[c][:, r]), in0=flat(heads_pre[c][:, 1, r]), scalar=0.0,
                in1=eps_sb[:, c, r.start * L : r.stop * L], op0=ALU.max, op1=ALU.mult,
            )

        def sample(c, r=slice(0, ROW_TILES)):
            nc.vector.scalar_tensor_tensor(
                out=flat(results[c][:, 2, r]), in0=flat(heads_pre[c][:, 0, r]), scalar=0.0,
                in1=flat(scaled[c][:, r]), op0=ALU.max, op1=ALU.add,
            )

        def store_out(c, s, r=slice(0, ROW_TILES)):
            out = (out_0, out_1, out_2)[s]
            rows = slice(c * CHUNK, (c + 1) * CHUNK)
            nc.sync.dma_start(
                out=out[rows, :].rearrange("(p r) l -> p r l", r=ROW_TILES)[:, r, :], in_=results[c][:, s, r, :]
            )

        w1_codes = const.tile([P, PASSES, HID], U32, align_bytes=64)
        w1_scales = const.tile([P, PASSES, HID], U8, align_bytes=64)
        w1_grouped = {}
        w3_grouped = const.tile([P, PASSES, 2 * L, PACK], BF16, align_bytes=64)
        w3_codes = const.tile([P, PASSES * 2 * L], U32, align_bytes=64)
        w3_scales = const.tile([P, PASSES * 2 * L], U8, align_bytes=64)

        def within(quarter):
            return slice(0, HALF) if quarter is None else slice(quarter * HALF // 2, (quarter + 1) * HALF // 2)

        def regroup_w1(g, half, copy=nc.vector.tensor_copy, quarter=None):
            if (g, half) not in w1_grouped:
                w1_grouped[g, half] = stage.tile([P, HALF, PACK], BF16, name="w1_grouped%d" % half, align_bytes=64)
            cols = within(quarter)
            regroup(w1_grouped[g, half][:, cols], w1_raw[g, half][:, :, cols], copy)

        def quantise_w1(g, half, quarter=None):
            cols = within(quarter)
            to = slice(half * HALF + cols.start, half * HALF + cols.stop)
            nc.vector.quantize_mx(
                out=w1_codes[:, g, to].bitcast(FP8X4),
                scales=w1_scales[:, g, to],
                in_=w1_grouped[g, half][:, cols].rearrange("p c t -> p (c t)"),
            )

        row_halves = [slice(0, CHUNK // 2), slice(CHUNK // 2, CHUNK)]

        def windows(rows):
            return [slice(g * CHUNK + rows.start, g * CHUNK + rows.stop) for g in range(PASSES)]

        both = (nc.scalar.copy, nc.scalar.copy)
        shared = (nc.scalar.copy, nc.vector.tensor_copy)
        keep_warm(8)
        for quarter in range(2):
            regroup_w1(0, 0, nc.vector.tensor_copy, quarter)
        for quarter in range(2):
            quantise_w1(0, 0, quarter)
        transpose_x(0, both, (0,))
        keep_warm(2)

        b11_rows_f32 = const.tile([P, P], F32)
        nc.scalar.copy(out=b11_rows_f32[:], in_=b11_rows[:])
        regroup_w1(1, 0)
        quantise_x(0, windows(row_halves[0]))
        quantise_w1(1, 0)
        transpose_x(0, both, (1,))
        keep_warm(2)
        b11_bank = psum.tile([P, BANK], F32, name="b11_bank", tag="bank")
        nc.tensor.transpose(b11_bank[:, 0:P], b11_rows_f32[:], ident[:])
        b11_col = const.tile([P, HID_TILES], F32)
        nc.scalar.copy(out=b11_col[:], in_=b11_bank[:, 0:HID_TILES])
        for h in range(PACK):
            stage1_matmul(0, h, row_halves[0])
        quantise_x(0, windows(row_halves[1]))
        for h in range(PACK):
            stage1_matmul(0, h, row_halves[1])
            stage1_relu(0, h)
        regroup_w1(0, 1)
        regroup_w1(1, 1)
        quantise_w1(0, 1)
        quantise_w1(1, 1)
        transpose_x(1, shared)
        for h in range(PACK, HID_TILES):
            stage1(0, h)
        regroup_enc(0, 0)
        quantise_x(1)

        def quantise_w3():
            nc.vector.quantize_mx(
                out=w3_codes[:].bitcast(FP8X4),
                scales=w3_scales[:],
                in_=w3_grouped[:].rearrange("p g n t -> p (g n t)"),
            )

        b3_all = const.tile([P, 2, L], F32)

        def exists(c):
            return 0 <= c < N_CHUNKS

        last = N_CHUNKS - 1
        for c in range(1, N_CHUNKS):
            if exists(c + 1) and c > 1:
                transpose_x(c + 1, both)
            if exists(c - 3):
                scale_noise(c - 3)
            regroup_enc(c - 1, 1)
            if exists(c - 3) and c - 3 < N_CHUNKS // 2:
                relu_heads(c - 3)
            if exists(c - 3):
                sample(c - 3)
            if c == 1:
                for g2 in range(PASSES):
                    regroup(w3_grouped[:, g2], w3_raw[:, g2])
            if exists(c - 3):
                quantise_enc(c - 1)
            else:
                for g2 in range(PASSES):
                    quantise_enc(c - 1, g2)
            if c == 1:
                quantise_w3()
            elif exists(c + 1):
                quantise_x(c + 1)
            for h in range(PACK):
                stage1(c, h)
            if c == 1:
                transpose_x(2, shared)
            if exists(c - 3):
                if c - 3 >= N_CHUNKS // 2:
                    relu_heads(c - 3)
                for s in (1, 0, 2):
                    store_out(c - 3, s)
            if exists(c - 2):
                stage2(c - 2, 0)
                stage2(c - 2, 1)
            for h in range(PACK, HID_TILES):
                stage1(c, h)
            if c == 1:
                b3_bank = psum.tile([P, BANK], F32, name="b3_bank", tag="bank")
                nc.tensor.matmul(out=b3_bank[:, 0 : 2 * L], lhsT=ones[:], rhs=b3_row[:], start=True, stop=True)
                nc.scalar.copy(out=b3_all[:].rearrange("p s l -> p (s l)"), in_=b3_bank[:, 0 : 2 * L])
            if exists(c - 2):
                add_head_bias(c - 2, 0)
                add_head_bias(c - 2, 1)
            if c < last:
                regroup_enc(c, 0)
            if c == 1:
                quantise_x(2)

        a, b = N_CHUNKS - 3, N_CHUNKS - 2
        regroup_enc(last, 0, row_halves[0])
        regroup_enc(last, 0, row_halves[1], nc.scalar.copy)
        stage2(b, 0)
        stage2(b, 1)
        scale_noise(a)
        quantise_enc(last, 0)
        sample(a)
        regroup_enc(last, 1, row_halves[0])
        regroup_enc(last, 1, row_halves[1], nc.scalar.copy)
        relu_heads(a)
        for s in (2, 0, 1):
            store_out(a, s)
        add_head_bias(b, 0)
        quantise_enc(last, 1, row_halves[0])
        add_head_bias(b, 1)
        quantise_enc(last, 1, row_halves[1])
        stage2(last, 0)
        stage2(last, 1)
        relu_heads(b)
        scale_noise(b)
        add_head_bias(last, 0)
        sample(b)
        for s in (0, 1, 2):
            store_out(b, s)
        for p in range(2):
            r = pairs[p]
            scale_noise(last, r)
            if p == 0:
                add_head_bias(last, 1)
            relu_heads(last, r)
            sample(last, r)
            for s in (0, 1, 2):
                store_out(last, s, r)
